import numpy as np
import ml_dtypes


def mxq(x, axis, fmt="e4m3"):
    dtype, down = {"e4m3": (ml_dtypes.float8_e4m3fn, 7), "e5m2": (ml_dtypes.float8_e5m2, 14)}[fmt]
    v = np.moveaxis(np.asarray(x, np.float32).astype(ml_dtypes.bfloat16).astype(np.float64), axis, -1)
    blocks = v.reshape(v.shape[:-1] + (-1, 32))
    amax = np.abs(blocks).max(-1, keepdims=True)
    byte = np.maximum(np.where(amax > 0, np.frexp(amax)[1] - 1 + 127, 0) - down, 1)
    scale = np.exp2(byte - 127.0)
    codes = (blocks / scale).astype(np.float32).astype(dtype).astype(np.float64)
    return np.moveaxis((codes * scale).reshape(v.shape), -1, axis)


WIDE = False


def mx_kscale(k):
    if not WIDE:
        return np.ones(k)
    levels = np.array([10, -10, 5, -5, 0])
    a = np.random.permutation(np.resize(levels, k // 512 * 4)).reshape(k // 512, 4)
    idx = np.arange(k)
    return np.exp2(a[idx // 512, idx % 128 // 32])


BF16 = ml_dtypes.bfloat16


def bf(x):
    return np.asarray(x, np.float32).astype(BF16)


def f64(x):
    return np.asarray(x).astype(np.float64)


B, S, D = 128, 16, 512


def sigmoid(v):
    return 1.0 / (1.0 + np.exp(-v))


def setup_inputs():
    s, t = mx_kscale(D), mx_kscale(D)
    return {
        "inputs": bf(np.random.standard_normal((B, D)) * s),
        "h_state": bf((np.random.standard_normal((B, S, D)) * 0.5 * t).reshape(B, S * D)),
        "c_state": bf(np.random.standard_normal((B, S * D)) * 0.5),
        "c_upd": bf(np.random.standard_normal((B, S, D))),
        "kernel": bf(np.random.standard_normal((D, 3 * D)) / np.sqrt(D) / s[:, None]),
        "recurrent_kernel": bf(np.random.standard_normal((D, 3 * D)) / np.sqrt(D) / t[:, None]),
        "bias": bf(np.random.standard_normal(3 * D) * 0.3),
    }


def reference(inputs, h_state, c_state, c_upd, kernel, recurrent_kernel, bias):
    h_tm1 = f64(h_state).reshape(B, S, D)
    c_tm1 = f64(c_state).reshape(B, S, D)
    xz = mxq(f64(inputs), 1, "e4m3") @ mxq(f64(kernel), 0, "e4m3")
    hz = mxq(h_tm1, 2, "e4m3") @ mxq(f64(recurrent_kernel), 0, "e4m3")
    z = xz[:, None, :] + hz + f64(bias)
    i = sigmoid(z[..., :D])
    f = sigmoid(z[..., D:2 * D])
    o = sigmoid(z[..., 2 * D:])
    c_new = f * c_tm1 + i * np.tanh(f64(c_upd))
    h_new = o * np.tanh(c_new)
    return h_new.reshape(B, -1), c_new.reshape(B, -1)

@@ -1,0 +1,291 @@
+from contextlib import ExitStack
+
+import concourse.mybir as mybir
+from concourse.masks import make_identity
+
+F32 = mybir.dt.float32
+BF16 = mybir.dt.bfloat16
+U32 = mybir.dt.uint32
+U8 = mybir.dt.uint8
+FP8X4 = mybir.dt.float8_e4m3fn_x4
+SIGMOID = mybir.ActivationFunctionType.Sigmoid
+TANH = mybir.ActivationFunctionType.Tanh
+MULT = mybir.AluOpType.mult
+ADD = mybir.AluOpType.add
+
+P = 128
+BATCH = 128
+SLOTS = 16
+D = 512
+GATES = 3
+PACK = 4
+HALVES = 2
+GROUP = 4
+GROUPS = SLOTS // GROUP
+BLOCKS = D // P
+MOVING = GROUP * BATCH
+
+FLOPS = 2 * (BATCH + BATCH * SLOTS) * D * GATES * D
+
+
+def tile_rlstmcell_pb_kernel(
+    tc, inputs, h_state, c_state, c_upd, kernel, recurrent_kernel, bias, out_0, out_1
+):
+    nc = tc.nc
+    with ExitStack() as ctx:
+        const = ctx.enter_context(tc.tile_pool(name="const", bufs=1))
+        resident = ctx.enter_context(tc.tile_pool(name="resident", bufs=1))
+        stage = ctx.enter_context(tc.tile_pool(name="stage", bufs=2))
+        gate_pool = ctx.enter_context(tc.tile_pool(name="gate_pool", bufs=2 * BLOCKS))
+        work = ctx.enter_context(tc.tile_pool(name="work", bufs=2))
+        z_psum = ctx.enter_context(tc.psum_pool(name="z_psum", bufs=4))
+        t_psum = ctx.enter_context(tc.psum_pool(name="t_psum", bufs=4))
+
+        weights = {"r": recurrent_kernel, "k": kernel}
+        w_raw, h_sb, c_sb, cu_sb = {}, {}, {}, {}
+
+        def load_weights(g):
+            for w in ("r", "k"):
+                w_raw[(w, g)] = resident.tile([P, PACK, D], BF16, name="raw_%s%d" % (w, g))
+                for u in range(HALVES):
+                    rows = weights[w][u * 2 * P : (u + 1) * 2 * P, g * D : (g + 1) * D]
+                    nc.sync.dma_start(
+                        out=w_raw[(w, g)][:, 2 * u : 2 * u + 2, :],
+                        in_=rows.rearrange("(p e) c -> p e c", e=2),
+                    )
+
+        def load_h(t):
+            h_sb[t] = resident.tile([P, GROUP * D], BF16, name="h_sb%d" % t)
+            nc.sync.dma_start(out=h_sb[t][:], in_=h_state[:, t * GROUP * D : (t + 1) * GROUP * D])
+
+        def load_candidate(t):
+            cu_sb[t] = resident.tile([P, GROUP, D], BF16, name="cu_sb%d" % t)
+            nc.sync.dma_start(out=cu_sb[t][:], in_=c_upd[:, t * GROUP : (t + 1) * GROUP, :])
+
+        def load_cell(t):
+            c_sb[t] = resident.tile([P, GROUP, D], BF16, name="c_sb%d" % t)
+            nc.sync.dma_start(
+                out=c_sb[t][:],
+                in_=c_state[:, t * GROUP * D : (t + 1) * GROUP * D].rearrange(
+                    "b (s d) -> b s d", s=GROUP
+                ),
+            )
+
+        bias_rows = const.tile([P, P], BF16, name="bias_rows")
+        nc.vector.memset(bias_rows[:], 0.0)
+        nc.scalar.dma_start(
+            out=bias_rows[0 : GATES * BLOCKS, :], in_=bias.rearrange("(m p) -> m p", p=P)
+        )
+
+        x_sb = resident.tile([P, D], BF16, name="x_sb")
+        nc.sync.dma_start(out=x_sb[:], in_=inputs)
+        load_h(0)
+        load_weights(0)
+        load_weights(1)
+        load_h(1)
+        load_candidate(0)
+        load_weights(2)
+        load_cell(0)
+        for t in range(1, GROUPS):
+            if t + 1 < GROUPS:
+                load_h(t + 1)
+            load_candidate(t)
+            load_cell(t)
+
+        warm = const.tile([P, 1], F32, name="warm")
+        nc.vector.memset(warm[:], 0.0)
+        nc.scalar.activation(out=warm[:], in_=warm[:], func=SIGMOID)
+
+        ident = const.tile([P, P], F32, name="ident")
+        make_identity(nc, ident[:])
+
+        xT_ps = t_psum.tile([P, MOVING], F32, name="xT_ps", tag="t")
+        x_words = x_sb[:].bitcast(F32)
+        for u in range(HALVES):
+            nc.tensor.transpose(xT_ps[:, u * P : (u + 1) * P], x_words[:, u * P : (u + 1) * P], ident[:])
+        xT_grouped = resident.tile([P, MOVING * PACK], BF16, name="xT_grouped", align_bytes=64)
+        nc.scalar.copy(
+            out=xT_grouped[:].bitcast(F32).rearrange("p (s b u) -> p s b u", s=GROUP, u=HALVES),
+            in_=xT_ps[:, 0 : HALVES * P]
+            .rearrange("p (u b) -> p b u", u=HALVES)
+            .unsqueeze(1)
+            .to_broadcast([P, GROUP, BATCH, HALVES]),
+        )
+        xT_codes = resident.tile([P, MOVING], U32, name="xT_codes", align_bytes=64)
+        xT_scales = resident.tile([P, MOVING], U8, name="xT_scales", align_bytes=64)
+
+        bias_rows_f32 = const.tile([P, P], F32, name="bias_rows_f32")
+        nc.vector.tensor_copy(out=bias_rows_f32[:], in_=bias_rows[:])
+        bias_ps = t_psum.tile([P, MOVING], F32, name="bias_ps", tag="t")
+        nc.tensor.transpose(bias_ps[:, 0:P], bias_rows_f32[:], ident[:])
+        bias_cols = const.tile([P, GATES * BLOCKS], F32, name="bias_cols")
+        nc.scalar.copy(out=bias_cols[:], in_=bias_ps[:, 0 : GATES * BLOCKS])
+
+        hT_grouped, hT_codes, hT_scales = {}, {}, {}
+
+        def transpose_h(t, pair, copy):
+            if pair == 0:
+                hT_grouped[t] = stage.tile(
+                    [P, MOVING * PACK], BF16, name="hT_grouped", align_bytes=64
+                )
+            h_words = h_sb[t][:].bitcast(F32)
+            hT_ps = t_psum.tile([P, MOVING], F32, name="hT_ps", tag="t")
+            for u in range(HALVES):
+                for j in range(2):
+                    first = ((2 * pair + j) * HALVES + u) * P
+                    nc.tensor.transpose(
+                        hT_ps[:, (2 * u + j) * P : (2 * u + j + 1) * P],
+                        h_words[:, first : first + P],
+                        ident[:],
+                    )
+            copy(
+                out=hT_grouped[t][:]
+                .bitcast(F32)[:, pair * MOVING : (pair + 1) * MOVING]
+                .rearrange("p (c u) -> p c u", u=HALVES),
+                in_=hT_ps[:].rearrange("p (u c) -> p c u", u=HALVES),
+            )
+
+        def quantise_h(t):
+            hT_codes[t] = stage.tile([P, MOVING], U32, name="hT_codes", align_bytes=64)
+            hT_scales[t] = stage.tile([P, MOVING], U8, name="hT_scales", align_bytes=64)
+            nc.vector.quantize_mx(
+                out=hT_codes[t][:].bitcast(FP8X4), scales=hT_scales[t][:], in_=hT_grouped[t][:]
+            )
+
+        w_grouped = {}
+        w_codes = {w: resident.tile([P, GATES * D], U32, name="codes_" + w, align_bytes=64) for w in weights}
+        w_scales = {w: resident.tile([P, GATES * D], U8, name="scales_" + w, align_bytes=64) for w in weights}
+
+        def regroup_weights(g):
+            for w in ("r", "k"):
+                w_grouped[w] = stage.tile([P, D, PACK], BF16, name="grouped_" + w, align_bytes=64)
+                nc.vector.tensor_copy(
+                    out=w_grouped[w][:].rearrange("p (c i) t -> p c t i", i=4),
+                    in_=w_raw[(w, g)][:].rearrange("p t (c i) -> p c t i", i=4),
+                )
+
+        def quantise_weights(g):
+            for w in ("r", "k"):
+                nc.vector.quantize_mx(
+                    out=w_codes[w][:, g * D : (g + 1) * D].bitcast(FP8X4),
+                    scales=w_scales[w][:, g * D : (g + 1) * D],
+                    in_=w_grouped[w][:].rearrange("p c t -> p (c t)"),
+                )
+
+        def block(tile3, q):
+            return tile3[:, :, q * P : (q + 1) * P]
+
+        def preactivation(t, g, q):
+            cols = slice((g * BLOCKS + q) * P, (g * BLOCKS + q + 1) * P)
+            z = z_psum.tile([P, MOVING], F32, name="z")
+            nc.tensor.matmul_mx(
+                out=z[:],
+                lhsT=w_codes["r"][:, cols].bitcast(FP8X4),
+                lhsT_scale=w_scales["r"][:, cols],
+                rhs=hT_codes[t][:].bitcast(FP8X4),
+                rhs_scale=hT_scales[t][:],
+                start=True,
+                stop=False,
+            )
+            nc.tensor.matmul_mx(
+                out=z[:],
+                lhsT=w_codes["k"][:, cols].bitcast(FP8X4),
+                lhsT_scale=w_scales["k"][:, cols],
+                rhs=xT_codes[:].bitcast(FP8X4),
+                rhs_scale=xT_scales[:],
+                start=False,
+                stop=True,
+            )
+            return z
+
+        def sigmoid(z, g, q):
+            gateT = gate_pool.tile([P, MOVING], F32, name="gateT")
+            m = g * BLOCKS + q
+            nc.scalar.activation(
+                out=gateT[:], in_=z[:], func=SIGMOID, bias=bias_cols[:, m : m + 1], scale=1.0
+            )
+            return gateT
+
+        def to_batch_rows(gateT):
+            gate = t_psum.tile([P, GROUP * P], F32, name="gate", tag="t")
+            for s in range(GROUP):
+                nc.tensor.transpose(gate[:, s * P : (s + 1) * P], gateT[:, s * P : (s + 1) * P], ident[:])
+            return gate[:].rearrange("b (s d) -> b s d", s=GROUP)
+
+        cand, keep, c_new, tanh_c, h_new = {}, {}, {}, {}, {}
+
+        def tanh_candidate(t, first_slot, slots):
+            if first_slot == 0:
+                cand[t] = work.tile([P, GROUP, D], F32, name="cand")
+            part = slice(first_slot, first_slot + slots)
+            nc.scalar.activation(out=cand[t][:, part, :], in_=cu_sb[t][:, part, :], func=TANH)
+
+        def apply_gate(t, g, q, gate):
+            if g == 0:
+                nc.vector.tensor_tensor(out=block(cand[t], q), in0=gate, in1=block(cand[t], q), op=MULT)
+            if g == 1:
+                if q == 0:
+                    keep[t] = work.tile([P, GROUP, D], F32, name="keep")
+                    c_new[t] = work.tile([P, GROUP, D], F32, name="c_new")
+                nc.vector.tensor_tensor(out=block(keep[t], q), in0=gate, in1=block(c_sb[t], q), op=MULT)
+                nc.gpsimd.tensor_tensor(
+                    out=block(c_new[t], q), in0=block(keep[t], q), in1=block(cand[t], q), op=ADD
+                )
+            if g == 2:
+                if q == 0:
+                    h_new[t] = work.tile([P, GROUP, D], F32, name="h_new")
+                nc.vector.tensor_tensor(out=block(h_new[t], q), in0=gate, in1=block(tanh_c[t], q), op=MULT)
+
+        def tanh_cell(t, q):
+            if q == 0:
+                tanh_c[t] = work.tile([P, GROUP, D], F32, name="tanh_c")
+            nc.scalar.activation(out=block(tanh_c[t], q), in_=block(c_new[t], q), func=TANH)
+
+        def store(out, t, tile3):
+            nc.sync.dma_start(
+                out=out[:, t * GROUP * D : (t + 1) * GROUP * D],
+                in_=tile3[:].rearrange("b s d -> b (s d)"),
+            )
+
+        transpose_h(0, 0, nc.scalar.copy)
+        transpose_h(0, 1, nc.scalar.copy)
+        nc.vector.quantize_mx(out=xT_codes[:].bitcast(FP8X4), scales=xT_scales[:], in_=xT_grouped[:])
+        regroup_weights(0)
+        quantise_h(0)
+        quantise_weights(0)
+
+        rounds = [(t, g) for t in range(GROUPS) for g in range(GATES)]
+        gatesT = {}
+        for r in range(len(rounds) + 1):
+            if r < len(rounds):
+                t, g = rounds[r]
+                zs = [preactivation(t, g, q) for q in range(BLOCKS)]
+                if t == 0 and g + 1 < GATES:
+                    regroup_weights(g + 1)
+                    quantise_weights(g + 1)
+                for q in range(BLOCKS):
+                    gatesT[(r, q)] = sigmoid(zs[q], g, q)
+                    if g == 0 and t > 0:
+                        tanh_cell(t - 1, q)
+                if r == 0:
+                    tanh_candidate(0, 0, GROUP)
+                if g > 0 and t + 1 < GROUPS:
+                    tanh_candidate(t + 1, (g - 1) * 2, 2)
+            else:
+                for q in range(BLOCKS):
+                    tanh_cell(GROUPS - 1, q)
+            if r > 0:
+                t_done, g_done = rounds[r - 1]
+                for q in range(BLOCKS):
+                    apply_gate(t_done, g_done, q, to_batch_rows(gatesT[(r - 1, q)]))
+                if g_done == 1:
+                    store(out_1, t_done, c_new[t_done])
+                if g_done == 2:
+                    store(out_0, t_done, h_new[t_done])
+            if r < len(rounds):
+                t, g = rounds[r]
+                if t + 1 < GROUPS:
+                    if g < 2:
+                        transpose_h(t + 1, g, nc.vector.tensor_copy)
+                    else:
+                        quantise_h(t + 1)

@@ -33,6 +33,7 @@ def tile_rlstmcell_pb_kernel(
 ):
     nc = tc.nc
     with ExitStack() as ctx:
+        ctx.enter_context(tc.manual_schedule())
         const = ctx.enter_context(tc.tile_pool(name="const", bufs=1))
         resident = ctx.enter_context(tc.tile_pool(name="resident", bufs=1))
         stage = ctx.enter_context(tc.tile_pool(name="stage", bufs=2))

@@ -18,6 +18,9 @@ BATCH = 128
 SLOTS = 16
 D = 512
 GATES = 3
+INPUT_GATE = 0
+FORGET_GATE = 1
+OUTPUT_GATE = 2
 PACK = 4
 HALVES = 2
 GROUP = 4
@@ -33,7 +36,6 @@ def tile_rlstmcell_pb_kernel(
 ):
     nc = tc.nc
     with ExitStack() as ctx:
-        ctx.enter_context(tc.manual_schedule())
         const = ctx.enter_context(tc.tile_pool(name="const", bufs=1))
         resident = ctx.enter_context(tc.tile_pool(name="resident", bufs=1))
         stage = ctx.enter_context(tc.tile_pool(name="stage", bufs=2))
@@ -77,21 +79,31 @@ def tile_rlstmcell_pb_kernel(
         nc.scalar.dma_start(
             out=bias_rows[0 : GATES * BLOCKS, :], in_=bias.rearrange("(m p) -> m p", p=P)
         )
+        bias_row0 = const.tile([P, D], BF16, name="bias_row0")
+        nc.vector.memset(bias_row0[:], 0.0)
+        nc.scalar.dma_start(
+            out=bias_row0[0:1, :],
+            in_=bias[INPUT_GATE * D : (INPUT_GATE + 1) * D].rearrange("(o d) -> o d", o=1),
+        )
+        ones = const.tile([P, P], BF16, name="ones")
+        nc.vector.memset(ones[:], 1.0)
 
         x_sb = resident.tile([P, D], BF16, name="x_sb")
         nc.sync.dma_start(out=x_sb[:], in_=inputs)
         load_h(0)
-        load_weights(0)
-        load_weights(1)
-        load_h(1)
+        load_weights(INPUT_GATE)
         load_candidate(0)
-        load_weights(2)
+        load_weights(FORGET_GATE)
+        load_candidate(1)
+        load_weights(OUTPUT_GATE)
         load_cell(0)
+        load_h(1)
+        load_candidate(2)
+        load_candidate(3)
         for t in range(1, GROUPS):
+            load_cell(t)
             if t + 1 < GROUPS:
                 load_h(t + 1)
-            load_candidate(t)
-            load_cell(t)
 
         warm = const.tile([P, 1], F32, name="warm")
         nc.vector.memset(warm[:], 0.0)
@@ -121,6 +133,11 @@ def tile_rlstmcell_pb_kernel(
         nc.tensor.transpose(bias_ps[:, 0:P], bias_rows_f32[:], ident[:])
         bias_cols = const.tile([P, GATES * BLOCKS], F32, name="bias_cols")
         nc.scalar.copy(out=bias_cols[:], in_=bias_ps[:, 0 : GATES * BLOCKS])
+
+        bias_all_ps = t_psum.tile([P, D], F32, name="bias_all_ps", tag="t")
+        nc.tensor.matmul(out=bias_all_ps[:], lhsT=ones[:], rhs=bias_row0[:], start=True, stop=True)
+        bias_all = const.tile([P, D], F32, name="bias_all")
+        nc.scalar.copy(out=bias_all[:], in_=bias_all_ps[:])
 
         hT_grouped, hT_codes, hT_scales = {}, {}, {}
 
@@ -173,39 +190,62 @@ def tile_rlstmcell_pb_kernel(
                     in_=w_grouped[w][:].rearrange("p c t -> p (c t)"),
                 )
 
+        def mx_pass(out, stationary, s_cols, moving, m_cols, start, stop):
+            nc.tensor.matmul_mx(
+                out=out,
+                lhsT=stationary[0][:, s_cols].bitcast(FP8X4),
+                lhsT_scale=stationary[1][:, s_cols],
+                rhs=moving[0][:, m_cols].bitcast(FP8X4),
+                rhs_scale=moving[1][:, m_cols],
+                start=start,
+                stop=stop,
+            )
+
+        whole = slice(0, MOVING)
+        x_mx = (xT_codes, xT_scales)
+        r_mx = (w_codes["r"], w_scales["r"])
+        k_mx = (w_codes["k"], w_scales["k"])
+        cand, gate_i, cell, tanh_c = {}, {}, {}, {}
+
         def block(tile3, q):
             return tile3[:, :, q * P : (q + 1) * P]
 
-        def preactivation(t, g, q):
-            cols = slice((g * BLOCKS + q) * P, (g * BLOCKS + q + 1) * P)
-            z = z_psum.tile([P, MOVING], F32, name="z")
-            nc.tensor.matmul_mx(
-                out=z[:],
-                lhsT=w_codes["r"][:, cols].bitcast(FP8X4),
-                lhsT_scale=w_scales["r"][:, cols],
-                rhs=hT_codes[t][:].bitcast(FP8X4),
-                rhs_scale=hT_scales[t][:],
-                start=True,
-                stop=False,
-            )
-            nc.tensor.matmul_mx(
-                out=z[:],
-                lhsT=w_codes["k"][:, cols].bitcast(FP8X4),
-                lhsT_scale=w_scales["k"][:, cols],
-                rhs=xT_codes[:].bitcast(FP8X4),
-                rhs_scale=xT_scales[:],
-                start=False,
-                stop=True,
-            )
-            return z
+        def tanh_candidate(t):
+            cand[t] = work.tile([P, GROUP, D], F32, name="cand", bufs=GROUPS)
+            for half in range(2):
+                part = slice(2 * half, 2 * half + 2)
+                nc.scalar.activation(out=cand[t][:, part, :], in_=cu_sb[t][:, part, :], func=TANH)
 
-        def sigmoid(z, g, q):
-            gateT = gate_pool.tile([P, MOVING], F32, name="gateT")
-            m = g * BLOCKS + q
-            nc.scalar.activation(
-                out=gateT[:], in_=z[:], func=SIGMOID, bias=bias_cols[:, m : m + 1], scale=1.0
-            )
-            return gateT
+        def input_gate(t):
+            i_cols = slice(INPUT_GATE * D, (INPUT_GATE + 1) * D)
+            gate_i[t] = work.tile([P, GROUP, D], F32, name="gate_i")
+            for s in range(GROUP):
+                hz = z_psum.tile([P, D], F32, name="hz", tag="z")
+                mx_pass(hz[:], (hT_codes[t], hT_scales[t]), slice(s * BATCH, (s + 1) * BATCH), r_mx, i_cols, True, True)
+                nc.vector.tensor_tensor(out=gate_i[t][:, s, :], in0=hz[:], in1=xz_bias[:], op=ADD)
+            for s in range(GROUP):
+                nc.scalar.activation(out=gate_i[t][:, s, :], in_=gate_i[t][:, s, :], func=SIGMOID)
+                nc.gpsimd.tensor_tensor(
+                    out=cand[t][:, s, :], in0=gate_i[t][:, s, :], in1=cand[t][:, s, :], op=MULT
+                )
+
+        def transposed_gate(t, g):
+            zs = []
+            for q in range(BLOCKS):
+                cols = slice((g * BLOCKS + q) * P, (g * BLOCKS + q + 1) * P)
+                z = z_psum.tile([P, MOVING], F32, name="z", tag="z")
+                mx_pass(z[:], r_mx, cols, (hT_codes[t], hT_scales[t]), whole, True, False)
+                mx_pass(z[:], k_mx, cols, x_mx, whole, False, True)
+                zs.append(z)
+            blocksT = []
+            for q in range(BLOCKS):
+                gateT = gate_pool.tile([P, MOVING], F32, name="gateT")
+                m = g * BLOCKS + q
+                nc.scalar.activation(
+                    out=gateT[:], in_=zs[q][:], func=SIGMOID, bias=bias_cols[:, m : m + 1], scale=1.0
+                )
+                blocksT.append(gateT)
+            return blocksT
 
         def to_batch_rows(gateT):
             gate = t_psum.tile([P, GROUP * P], F32, name="gate", tag="t")
@@ -213,80 +253,73 @@ def tile_rlstmcell_pb_kernel(
                 nc.tensor.transpose(gate[:, s * P : (s + 1) * P], gateT[:, s * P : (s + 1) * P], ident[:])
             return gate[:].rearrange("b (s d) -> b s d", s=GROUP)
 
-        cand, keep, c_new, tanh_c, h_new = {}, {}, {}, {}, {}
-
-        def tanh_candidate(t, first_slot, slots):
-            if first_slot == 0:
-                cand[t] = work.tile([P, GROUP, D], F32, name="cand")
-            part = slice(first_slot, first_slot + slots)
-            nc.scalar.activation(out=cand[t][:, part, :], in_=cu_sb[t][:, part, :], func=TANH)
-
-        def apply_gate(t, g, q, gate):
-            if g == 0:
-                nc.vector.tensor_tensor(out=block(cand[t], q), in0=gate, in1=block(cand[t], q), op=MULT)
-            if g == 1:
-                if q == 0:
-                    keep[t] = work.tile([P, GROUP, D], F32, name="keep")
-                    c_new[t] = work.tile([P, GROUP, D], F32, name="c_new")
-                nc.vector.tensor_tensor(out=block(keep[t], q), in0=gate, in1=block(c_sb[t], q), op=MULT)
-                nc.gpsimd.tensor_tensor(
-                    out=block(c_new[t], q), in0=block(keep[t], q), in1=block(cand[t], q), op=ADD
-                )
-            if g == 2:
-                if q == 0:
-                    h_new[t] = work.tile([P, GROUP, D], F32, name="h_new")
-                nc.vector.tensor_tensor(out=block(h_new[t], q), in0=gate, in1=block(tanh_c[t], q), op=MULT)
-
-        def tanh_cell(t, q):
-            if q == 0:
-                tanh_c[t] = work.tile([P, GROUP, D], F32, name="tanh_c")
-            nc.scalar.activation(out=block(tanh_c[t], q), in_=block(c_new[t], q), func=TANH)
-
         def store(out, t, tile3):
             nc.sync.dma_start(
                 out=out[:, t * GROUP * D : (t + 1) * GROUP * D],
                 in_=tile3[:].rearrange("b s d -> b (s d)"),
             )
 
+        def store_block(out, t, tile3, q):
+            group_cols = out[:, t * GROUP * D : (t + 1) * GROUP * D].rearrange("b (s d) -> b s d", s=GROUP)
+            nc.sync.dma_start(out=block(group_cols, q), in_=block(tile3, q))
+
+        last = GROUPS - 1
+
+        def new_cell(t, forgetT):
+            cell[t] = work.tile([P, GROUP, D], F32, name="cell")
+            tanh_c[t] = work.tile([P, GROUP, D], F32, name="tanh_c")
+            for q in range(BLOCKS):
+                nc.vector.tensor_tensor(
+                    out=block(cell[t], q), in0=to_batch_rows(forgetT[q]), in1=block(c_sb[t], q), op=MULT
+                )
+                adder = nc.vector if t == last else nc.gpsimd
+                adder.tensor_tensor(
+                    out=block(cell[t], q), in0=block(cell[t], q), in1=block(cand[t], q), op=ADD
+                )
+                nc.scalar.activation(out=block(tanh_c[t], q), in_=block(cell[t], q), func=TANH)
+            store(out_1, t, cell[t])
+
+        def new_h(t, outputT):
+            for q in range(BLOCKS):
+                nc.vector.tensor_tensor(
+                    out=block(tanh_c[t], q), in0=to_batch_rows(outputT[q]), in1=block(tanh_c[t], q), op=MULT
+                )
+                if t == last:
+                    store_block(out_0, t, tanh_c[t], q)
+            if t != last:
+                store(out_0, t, tanh_c[t])
+
         transpose_h(0, 0, nc.scalar.copy)
         transpose_h(0, 1, nc.scalar.copy)
         nc.vector.quantize_mx(out=xT_codes[:].bitcast(FP8X4), scales=xT_scales[:], in_=xT_grouped[:])
-        regroup_weights(0)
+        regroup_weights(INPUT_GATE)
         quantise_h(0)
-        quantise_weights(0)
+        quantise_weights(INPUT_GATE)
+        for t in range(GROUPS):
+            tanh_candidate(t)
 
-        rounds = [(t, g) for t in range(GROUPS) for g in range(GATES)]
-        gatesT = {}
-        for r in range(len(rounds) + 1):
-            if r < len(rounds):
-                t, g = rounds[r]
-                zs = [preactivation(t, g, q) for q in range(BLOCKS)]
-                if t == 0 and g + 1 < GATES:
-                    regroup_weights(g + 1)
-                    quantise_weights(g + 1)
-                for q in range(BLOCKS):
-                    gatesT[(r, q)] = sigmoid(zs[q], g, q)
-                    if g == 0 and t > 0:
-                        tanh_cell(t - 1, q)
-                if r == 0:
-                    tanh_candidate(0, 0, GROUP)
-                if g > 0 and t + 1 < GROUPS:
-                    tanh_candidate(t + 1, (g - 1) * 2, 2)
-            else:
-                for q in range(BLOCKS):
-                    tanh_cell(GROUPS - 1, q)
-            if r > 0:
-                t_done, g_done = rounds[r - 1]
-                for q in range(BLOCKS):
-                    apply_gate(t_done, g_done, q, to_batch_rows(gatesT[(r - 1, q)]))
-                if g_done == 1:
-                    store(out_1, t_done, c_new[t_done])
-                if g_done == 2:
-                    store(out_0, t_done, h_new[t_done])
-            if r < len(rounds):
-                t, g = rounds[r]
-                if t + 1 < GROUPS:
-                    if g < 2:
-                        transpose_h(t + 1, g, nc.vector.tensor_copy)
-                    else:
-                        quantise_h(t + 1)
+        xz_ps = z_psum.tile([P, D], F32, name="xz_ps", tag="z")
+        mx_pass(xz_ps[:], x_mx, slice(0, BATCH), k_mx, slice(INPUT_GATE * D, (INPUT_GATE + 1) * D), True, True)
+        xz_bias = const.tile([P, D], F32, name="xz_bias")
+        nc.vector.tensor_tensor(out=xz_bias[:], in0=xz_ps[:], in1=bias_all[:], op=ADD)
+
+        outputT = {}
+        for t in range(GROUPS):
+            input_gate(t)
+            if t == 0:
+                regroup_weights(FORGET_GATE)
+                quantise_weights(FORGET_GATE)
+            forgetT = transposed_gate(t, FORGET_GATE)
+            if t > 0:
+                new_h(t - 1, outputT[t - 1])
+            if t + 1 < GROUPS:
+                transpose_h(t + 1, 0, nc.vector.tensor_copy)
+                transpose_h(t + 1, 1, nc.vector.tensor_copy)
+            if t == 0:
+                regroup_weights(OUTPUT_GATE)
+                quantise_weights(OUTPUT_GATE)
+            outputT[t] = transposed_gate(t, OUTPUT_GATE)
+            if t + 1 < GROUPS:
+                quantise_h(t + 1)
+            new_cell(t, forgetT)
+        new_h(GROUPS - 1, outputT[GROUPS - 1])

from contextlib import ExitStack

import concourse.mybir as mybir
from concourse.masks import make_identity

F32 = mybir.dt.float32
BF16 = mybir.dt.bfloat16
U32 = mybir.dt.uint32
U8 = mybir.dt.uint8
FP8X4 = mybir.dt.float8_e4m3fn_x4
SIGMOID = mybir.ActivationFunctionType.Sigmoid
TANH = mybir.ActivationFunctionType.Tanh
MULT = mybir.AluOpType.mult
ADD = mybir.AluOpType.add

P = 128
BATCH = 128
SLOTS = 16
D = 512
GATES = 3
INPUT_GATE = 0
FORGET_GATE = 1
OUTPUT_GATE = 2
PACK = 4
HALVES = 2
GROUP = 4
GROUPS = SLOTS // GROUP
BLOCKS = D // P
MOVING = GROUP * BATCH

FLOPS = 2 * (BATCH + BATCH * SLOTS) * D * GATES * D


def tile_rlstmcell_pb_kernel(
    tc, inputs, h_state, c_state, c_upd, kernel, recurrent_kernel, bias, out_0, out_1
):
    nc = tc.nc
    with ExitStack() as ctx:
        const = ctx.enter_context(tc.tile_pool(name="const", bufs=1))
        resident = ctx.enter_context(tc.tile_pool(name="resident", bufs=1))
        stage = ctx.enter_context(tc.tile_pool(name="stage", bufs=2))
        gate_pool = ctx.enter_context(tc.tile_pool(name="gate_pool", bufs=2 * BLOCKS))
        work = ctx.enter_context(tc.tile_pool(name="work", bufs=2))
        z_psum = ctx.enter_context(tc.psum_pool(name="z_psum", bufs=4))
        t_psum = ctx.enter_context(tc.psum_pool(name="t_psum", bufs=4))

        weights = {"r": recurrent_kernel, "k": kernel}
        w_raw, h_sb, c_sb, cu_sb = {}, {}, {}, {}

        def load_weights(g):
            for w in ("r", "k"):
                w_raw[(w, g)] = resident.tile([P, PACK, D], BF16, name="raw_%s%d" % (w, g))
                for u in range(HALVES):
                    rows = weights[w][u * 2 * P : (u + 1) * 2 * P, g * D : (g + 1) * D]
                    nc.sync.dma_start(
                        out=w_raw[(w, g)][:, 2 * u : 2 * u + 2, :],
                        in_=rows.rearrange("(p e) c -> p e c", e=2),
                    )

        def load_h(t):
            h_sb[t] = resident.tile([P, GROUP * D], BF16, name="h_sb%d" % t)
            nc.sync.dma_start(out=h_sb[t][:], in_=h_state[:, t * GROUP * D : (t + 1) * GROUP * D])

        def load_candidate(t):
            cu_sb[t] = resident.tile([P, GROUP, D], BF16, name="cu_sb%d" % t)
            nc.sync.dma_start(out=cu_sb[t][:], in_=c_upd[:, t * GROUP : (t + 1) * GROUP, :])

        def load_cell(t):
            c_sb[t] = resident.tile([P, GROUP, D], BF16, name="c_sb%d" % t)
            nc.sync.dma_start(
                out=c_sb[t][:],
                in_=c_state[:, t * GROUP * D : (t + 1) * GROUP * D].rearrange(
                    "b (s d) -> b s d", s=GROUP
                ),
            )

        bias_rows = const.tile([P, P], BF16, name="bias_rows")
        nc.vector.memset(bias_rows[:], 0.0)
        nc.scalar.dma_start(
            out=bias_rows[0 : GATES * BLOCKS, :], in_=bias.rearrange("(m p) -> m p", p=P)
        )
        bias_row0 = const.tile([P, D], BF16, name="bias_row0")
        nc.vector.memset(bias_row0[:], 0.0)
        nc.scalar.dma_start(
            out=bias_row0[0:1, :],
            in_=bias[INPUT_GATE * D : (INPUT_GATE + 1) * D].rearrange("(o d) -> o d", o=1),
        )
        ones = const.tile([P, P], BF16, name="ones")
        nc.vector.memset(ones[:], 1.0)

        x_sb = resident.tile([P, D], BF16, name="x_sb")
        nc.sync.dma_start(out=x_sb[:], in_=inputs)
        load_h(0)
        load_weights(INPUT_GATE)
        load_candidate(0)
        load_weights(FORGET_GATE)
        load_candidate(1)
        load_weights(OUTPUT_GATE)
        load_cell(0)
        load_h(1)
        load_candidate(2)
        load_candidate(3)
        for t in range(1, GROUPS):
            load_cell(t)
            if t + 1 < GROUPS:
                load_h(t + 1)

        warm = const.tile([P, 1], F32, name="warm")
        nc.vector.memset(warm[:], 0.0)
        nc.scalar.activation(out=warm[:], in_=warm[:], func=SIGMOID)

        ident = const.tile([P, P], F32, name="ident")
        make_identity(nc, ident[:])

        xT_ps = t_psum.tile([P, MOVING], F32, name="xT_ps", tag="t")
        x_words = x_sb[:].bitcast(F32)
        for u in range(HALVES):
            nc.tensor.transpose(xT_ps[:, u * P : (u + 1) * P], x_words[:, u * P : (u + 1) * P], ident[:])
        xT_grouped = resident.tile([P, MOVING * PACK], BF16, name="xT_grouped", align_bytes=64)
        nc.scalar.copy(
            out=xT_grouped[:].bitcast(F32).rearrange("p (s b u) -> p s b u", s=GROUP, u=HALVES),
            in_=xT_ps[:, 0 : HALVES * P]
            .rearrange("p (u b) -> p b u", u=HALVES)
            .unsqueeze(1)
            .to_broadcast([P, GROUP, BATCH, HALVES]),
        )
        xT_codes = resident.tile([P, MOVING], U32, name="xT_codes", align_bytes=64)
        xT_scales = resident.tile([P, MOVING], U8, name="xT_scales", align_bytes=64)

        bias_rows_f32 = const.tile([P, P], F32, name="bias_rows_f32")
        nc.vector.tensor_copy(out=bias_rows_f32[:], in_=bias_rows[:])
        bias_ps = t_psum.tile([P, MOVING], F32, name="bias_ps", tag="t")
        nc.tensor.transpose(bias_ps[:, 0:P], bias_rows_f32[:], ident[:])
        bias_cols = const.tile([P, GATES * BLOCKS], F32, name="bias_cols")
        nc.scalar.copy(out=bias_cols[:], in_=bias_ps[:, 0 : GATES * BLOCKS])

        bias_all_ps = t_psum.tile([P, D], F32, name="bias_all_ps", tag="t")
        nc.tensor.matmul(out=bias_all_ps[:], lhsT=ones[:], rhs=bias_row0[:], start=True, stop=True)
        bias_all = const.tile([P, D], F32, name="bias_all")
        nc.scalar.copy(out=bias_all[:], in_=bias_all_ps[:])

        hT_grouped, hT_codes, hT_scales = {}, {}, {}

        def transpose_h(t, pair, copy):
            if pair == 0:
                hT_grouped[t] = stage.tile(
                    [P, MOVING * PACK], BF16, name="hT_grouped", align_bytes=64
                )
            h_words = h_sb[t][:].bitcast(F32)
            hT_ps = t_psum.tile([P, MOVING], F32, name="hT_ps", tag="t")
            for u in range(HALVES):
                for j in range(2):
                    first = ((2 * pair + j) * HALVES + u) * P
                    nc.tensor.transpose(
                        hT_ps[:, (2 * u + j) * P : (2 * u + j + 1) * P],
                        h_words[:, first : first + P],
                        ident[:],
                    )
            copy(
                out=hT_grouped[t][:]
                .bitcast(F32)[:, pair * MOVING : (pair + 1) * MOVING]
                .rearrange("p (c u) -> p c u", u=HALVES),
                in_=hT_ps[:].rearrange("p (u c) -> p c u", u=HALVES),
            )

        def quantise_h(t):
            hT_codes[t] = stage.tile([P, MOVING], U32, name="hT_codes", align_bytes=64)
            hT_scales[t] = stage.tile([P, MOVING], U8, name="hT_scales", align_bytes=64)
            nc.vector.quantize_mx(
                out=hT_codes[t][:].bitcast(FP8X4), scales=hT_scales[t][:], in_=hT_grouped[t][:]
            )

        w_grouped = {}
        w_codes = {w: resident.tile([P, GATES * D], U32, name="codes_" + w, align_bytes=64) for w in weights}
        w_scales = {w: resident.tile([P, GATES * D], U8, name="scales_" + w, align_bytes=64) for w in weights}

        def regroup_weights(g):
            for w in ("r", "k"):
                w_grouped[w] = stage.tile([P, D, PACK], BF16, name="grouped_" + w, align_bytes=64)
                nc.vector.tensor_copy(
                    out=w_grouped[w][:].rearrange("p (c i) t -> p c t i", i=4),
                    in_=w_raw[(w, g)][:].rearrange("p t (c i) -> p c t i", i=4),
                )

        def quantise_weights(g):
            for w in ("r", "k"):
                nc.vector.quantize_mx(
                    out=w_codes[w][:, g * D : (g + 1) * D].bitcast(FP8X4),
                    scales=w_scales[w][:, g * D : (g + 1) * D],
                    in_=w_grouped[w][:].rearrange("p c t -> p (c t)"),
                )

        def mx_pass(out, stationary, s_cols, moving, m_cols, start, stop):
            nc.tensor.matmul_mx(
                out=out,
                lhsT=stationary[0][:, s_cols].bitcast(FP8X4),
                lhsT_scale=stationary[1][:, s_cols],
                rhs=moving[0][:, m_cols].bitcast(FP8X4),
                rhs_scale=moving[1][:, m_cols],
                start=start,
                stop=stop,
            )

        whole = slice(0, MOVING)
        x_mx = (xT_codes, xT_scales)
        r_mx = (w_codes["r"], w_scales["r"])
        k_mx = (w_codes["k"], w_scales["k"])
        cand, gate_i, cell, tanh_c = {}, {}, {}, {}

        def block(tile3, q):
            return tile3[:, :, q * P : (q + 1) * P]

        def tanh_candidate(t):
            cand[t] = work.tile([P, GROUP, D], F32, name="cand", bufs=GROUPS)
            for half in range(2):
                part = slice(2 * half, 2 * half + 2)
                nc.scalar.activation(out=cand[t][:, part, :], in_=cu_sb[t][:, part, :], func=TANH)

        def input_gate(t):
            i_cols = slice(INPUT_GATE * D, (INPUT_GATE + 1) * D)
            gate_i[t] = work.tile([P, GROUP, D], F32, name="gate_i")
            for s in range(GROUP):
                hz = z_psum.tile([P, D], F32, name="hz", tag="z")
                mx_pass(hz[:], (hT_codes[t], hT_scales[t]), slice(s * BATCH, (s + 1) * BATCH), r_mx, i_cols, True, True)
                nc.vector.tensor_tensor(out=gate_i[t][:, s, :], in0=hz[:], in1=xz_bias[:], op=ADD)
            for s in range(GROUP):
                nc.scalar.activation(out=gate_i[t][:, s, :], in_=gate_i[t][:, s, :], func=SIGMOID)
                nc.gpsimd.tensor_tensor(
                    out=cand[t][:, s, :], in0=gate_i[t][:, s, :], in1=cand[t][:, s, :], op=MULT
                )

        def transposed_gate(t, g):
            zs = []
            for q in range(BLOCKS):
                cols = slice((g * BLOCKS + q) * P, (g * BLOCKS + q + 1) * P)
                z = z_psum.tile([P, MOVING], F32, name="z", tag="z")
                mx_pass(z[:], r_mx, cols, (hT_codes[t], hT_scales[t]), whole, True, False)
                mx_pass(z[:], k_mx, cols, x_mx, whole, False, True)
                zs.append(z)
            blocksT = []
            for q in range(BLOCKS):
                gateT = gate_pool.tile([P, MOVING], F32, name="gateT")
                m = g * BLOCKS + q
                nc.scalar.activation(
                    out=gateT[:], in_=zs[q][:], func=SIGMOID, bias=bias_cols[:, m : m + 1], scale=1.0
                )
                blocksT.append(gateT)
            return blocksT

        def to_batch_rows(gateT):
            gate = t_psum.tile([P, GROUP * P], F32, name="gate", tag="t")
            for s in range(GROUP):
                nc.tensor.transpose(gate[:, s * P : (s + 1) * P], gateT[:, s * P : (s + 1) * P], ident[:])
            return gate[:].rearrange("b (s d) -> b s d", s=GROUP)

        def store(out, t, tile3):
            nc.sync.dma_start(
                out=out[:, t * GROUP * D : (t + 1) * GROUP * D],
                in_=tile3[:].rearrange("b s d -> b (s d)"),
            )

        def store_block(out, t, tile3, q):
            group_cols = out[:, t * GROUP * D : (t + 1) * GROUP * D].rearrange("b (s d) -> b s d", s=GROUP)
            nc.sync.dma_start(out=block(group_cols, q), in_=block(tile3, q))

        last = GROUPS - 1

        def new_cell(t, forgetT):
            cell[t] = work.tile([P, GROUP, D], F32, name="cell")
            tanh_c[t] = work.tile([P, GROUP, D], F32, name="tanh_c")
            for q in range(BLOCKS):
                nc.vector.tensor_tensor(
                    out=block(cell[t], q), in0=to_batch_rows(forgetT[q]), in1=block(c_sb[t], q), op=MULT
                )
                adder = nc.vector if t == last else nc.gpsimd
                adder.tensor_tensor(
                    out=block(cell[t], q), in0=block(cell[t], q), in1=block(cand[t], q), op=ADD
                )
                nc.scalar.activation(out=block(tanh_c[t], q), in_=block(cell[t], q), func=TANH)
            store(out_1, t, cell[t])

        def new_h(t, outputT):
            for q in range(BLOCKS):
                nc.vector.tensor_tensor(
                    out=block(tanh_c[t], q), in0=to_batch_rows(outputT[q]), in1=block(tanh_c[t], q), op=MULT
                )
                if t == last:
                    store_block(out_0, t, tanh_c[t], q)
            if t != last:
                store(out_0, t, tanh_c[t])

        transpose_h(0, 0, nc.scalar.copy)
        transpose_h(0, 1, nc.scalar.copy)
        nc.vector.quantize_mx(out=xT_codes[:].bitcast(FP8X4), scales=xT_scales[:], in_=xT_grouped[:])
        regroup_weights(INPUT_GATE)
        quantise_h(0)
        quantise_weights(INPUT_GATE)
        for t in range(GROUPS):
            tanh_candidate(t)

        xz_ps = z_psum.tile([P, D], F32, name="xz_ps", tag="z")
        mx_pass(xz_ps[:], x_mx, slice(0, BATCH), k_mx, slice(INPUT_GATE * D, (INPUT_GATE + 1) * D), True, True)
        xz_bias = const.tile([P, D], F32, name="xz_bias")
        nc.vector.tensor_tensor(out=xz_bias[:], in0=xz_ps[:], in1=bias_all[:], op=ADD)

        outputT = {}
        for t in range(GROUPS):
            input_gate(t)
            if t == 0:
                regroup_weights(FORGET_GATE)
                quantise_weights(FORGET_GATE)
            forgetT = transposed_gate(t, FORGET_GATE)
            if t > 0:
                new_h(t - 1, outputT[t - 1])
            if t + 1 < GROUPS:
                transpose_h(t + 1, 0, nc.vector.tensor_copy)
                transpose_h(t + 1, 1, nc.vector.tensor_copy)
            if t == 0:
                regroup_weights(OUTPUT_GATE)
                quantise_weights(OUTPUT_GATE)
            outputT[t] = transposed_gate(t, OUTPUT_GATE)
            if t + 1 < GROUPS:
                quantise_h(t + 1)
            new_cell(t, forgetT)
        new_h(GROUPS - 1, outputT[GROUPS - 1])
